import numpy as np
import ml_dtypes

BF16 = ml_dtypes.bfloat16


def bf(x):
    return np.asarray(x, np.float32).astype(BF16)


def f32(x):
    return np.asarray(x, np.float32)


def f64(x):
    return np.asarray(x).astype(np.float64)


def striped(idx):
    return np.tile(idx.reshape(-1, 16).T, (8, 1))


C, S, N = 512, 512, 128


def silu(v):
    return v / (1.0 + np.exp(-v))


def setup_inputs():
    return {
        "ptab": f32(np.random.standard_normal((C, S))),
        "msgs": bf(np.random.standard_normal((C, N))),
        "w_msg": bf(np.random.standard_normal((C, C)) / np.sqrt(C)),
        "b1": f32(0.1 * np.random.standard_normal((C, 1))),
        "w2": bf(np.random.standard_normal((C, C)) / np.sqrt(C)),
        "b2": f32(0.1 * np.random.standard_normal((C, 1))),
        "offs": striped(np.random.permutation(np.tile(np.arange(S), 2))[:N]),
    }


def reference(ptab, msgs, w_msg, b1, w2, b2, offs):
    idx = offs[:16].T.reshape(-1)
    pre = f64(ptab)[:, idx] + f64(w_msg).T @ f64(msgs) + f64(b1)
    hid = silu(pre)
    return f64(w2).T @ hid + f64(b2)

@@ -1,0 +1,77 @@
+import concourse.mybir as mybir
+
+P = 128
+C = 512
+S = 512
+N = 128
+NB = C // P
+
+FLOPS = 2 * (2 * C * C * N)
+
+BF16, F32, U16 = mybir.dt.bfloat16, mybir.dt.float32, mybir.dt.uint16
+ADD = mybir.AluOpType.add
+SILU = mybir.ActivationFunctionType.Silu
+IDENTITY = mybir.ActivationFunctionType.Identity
+
+
+def block(i):
+    return slice(i * P, (i + 1) * P)
+
+
+def tile_cartesiantransformer_kernel(tc, ptab, msgs, w_msg, b1, w2, b2, offs, out):
+    nc = tc.nc
+    with (
+        tc.tile_pool(name="held", bufs=1) as held,
+        tc.psum_pool(name="psum", bufs=1) as psum,
+    ):
+        offsets = held.tile([P, N // 16], U16, name="offsets")
+        nc.sync.dma_start(offsets[:], offs)
+
+        msgs_sb = [held.tile([P, N], BF16, name=f"msgs_sb{k}") for k in range(NB)]
+        w_msg_sb = [held.tile([P, C], BF16, name=f"w_msg_sb{k}") for k in range(NB)]
+        ptab_sb = [held.tile([P, S], F32, name=f"ptab_sb{c}") for c in range(NB)]
+        w2_sb = [held.tile([P, C], BF16, name=f"w2_sb{c}") for c in range(NB)]
+        for k in range(NB):
+            nc.sync.dma_start(msgs_sb[k][:], msgs[block(k), :])
+            nc.sync.dma_start(w_msg_sb[k][:], w_msg[block(k), :])
+        for c in range(NB):
+            nc.scalar.dma_start(ptab_sb[c][:], ptab[block(c), :])
+        for c in range(NB):
+            nc.sync.dma_start(w2_sb[c][:], w2[block(c), :])
+
+        b1_sb = held.tile([P, NB], F32, name="b1_sb")
+        b2_sb = held.tile([P, NB], F32, name="b2_sb")
+        with nc.allow_non_contiguous_dma(reason="a bias of 512 values, one to a partition"):
+            nc.gpsimd.dma_start(b1_sb[:], b1.rearrange("(i p) o -> p (i o)", p=P))
+            nc.gpsimd.dma_start(b2_sb[:], b2.rearrange("(i p) o -> p (i o)", p=P))
+
+        proj = [psum.tile([P, N], F32, name=f"proj{c}") for c in range(NB)]
+        for k in range(NB):
+            for c in range(NB):
+                nc.tensor.matmul(
+                    proj[c][:], w_msg_sb[k][:, block(c)], msgs_sb[k][:],
+                    start=(k == 0), stop=(k == NB - 1),
+                )
+
+        acc = [psum.tile([P, N], F32, name=f"acc{m}") for m in range(NB)]
+        for c in range(NB):
+            proj_sb = held.tile([P, N], F32, name=f"proj_sb{c}")
+            nc.scalar.activation(proj_sb[:], proj[c][:], IDENTITY, bias=b1_sb[:, c : c + 1])
+            pre = held.tile([P, N], F32, name=f"pre{c}")
+            nc.vector.tensor_tensor(pre[:], ptab_sb[c][:].indirect(offsets[:]), proj_sb[:], ADD)
+            hid = held.tile([P, N], BF16, name=f"hid{c}")
+            nc.scalar.activation(hid[:], pre[:], SILU)
+            for m in range(NB):
+                nc.tensor.matmul(
+                    acc[m][:], w2_sb[c][:, block(m)], hid[:],
+                    start=(c == 0), stop=(c == NB - 1),
+                )
+
+        for m in range(NB):
+            out_sb = held.tile([P, N], F32, name=f"out_sb{m}")
+            if m % 2 == 0:
+                nc.vector.tensor_scalar_add(out_sb[:], acc[m][:], b2_sb[:, m : m + 1])
+                nc.sync.dma_start(out[block(m), :], out_sb[:])
+            else:
+                nc.scalar.activation(out_sb[:], acc[m][:], IDENTITY, bias=b2_sb[:, m : m + 1])
+                nc.scalar.dma_start(out[block(m), :], out_sb[:])

@@ -26,24 +26,30 @@ def tile_cartesiantransformer_kernel(tc, ptab, msgs, w_msg, b1, w2, b2, offs, ou
     ):
         offsets = held.tile([P, N // 16], U16, name="offsets")
         nc.sync.dma_start(offsets[:], offs)
+        queues = (nc.sync, nc.scalar)
 
         msgs_sb = [held.tile([P, N], BF16, name=f"msgs_sb{k}") for k in range(NB)]
         w_msg_sb = [held.tile([P, C], BF16, name=f"w_msg_sb{k}") for k in range(NB)]
         ptab_sb = [held.tile([P, S], F32, name=f"ptab_sb{c}") for c in range(NB)]
         w2_sb = [held.tile([P, C], BF16, name=f"w2_sb{c}") for c in range(NB)]
         for k in range(NB):
-            nc.sync.dma_start(msgs_sb[k][:], msgs[block(k), :])
-            nc.sync.dma_start(w_msg_sb[k][:], w_msg[block(k), :])
+            queues[k % 2].dma_start(msgs_sb[k][:], msgs[block(k), :])
+            queues[k % 2].dma_start(w_msg_sb[k][:], w_msg[block(k), :])
         for c in range(NB):
-            nc.scalar.dma_start(ptab_sb[c][:], ptab[block(c), :])
+            queues[c % 2].dma_start(ptab_sb[c][:], ptab[block(c), :])
         for c in range(NB):
-            nc.sync.dma_start(w2_sb[c][:], w2[block(c), :])
+            queues[c % 2].dma_start(w2_sb[c][:], w2[block(c), :])
 
         b1_sb = held.tile([P, NB], F32, name="b1_sb")
         b2_sb = held.tile([P, NB], F32, name="b2_sb")
         with nc.allow_non_contiguous_dma(reason="a bias of 512 values, one to a partition"):
             nc.gpsimd.dma_start(b1_sb[:], b1.rearrange("(i p) o -> p (i o)", p=P))
             nc.gpsimd.dma_start(b2_sb[:], b2.rearrange("(i p) o -> p (i o)", p=P))
+
+        scratch = held.tile([P, 1], F32, name="scratch")
+        scratch_silu = held.tile([P, 1], F32, name="scratch_silu")
+        nc.vector.memset(scratch[:], 0.0)
+        nc.scalar.activation(scratch_silu[:], scratch[:], SILU)
 
         proj = [psum.tile([P, N], F32, name=f"proj{c}") for c in range(NB)]
         for k in range(NB):

@@ -26,19 +26,18 @@ def tile_cartesiantransformer_kernel(tc, ptab, msgs, w_msg, b1, w2, b2, offs, ou
     ):
         offsets = held.tile([P, N // 16], U16, name="offsets")
         nc.sync.dma_start(offsets[:], offs)
-        queues = (nc.sync, nc.scalar)
 
         msgs_sb = [held.tile([P, N], BF16, name=f"msgs_sb{k}") for k in range(NB)]
         w_msg_sb = [held.tile([P, C], BF16, name=f"w_msg_sb{k}") for k in range(NB)]
         ptab_sb = [held.tile([P, S], F32, name=f"ptab_sb{c}") for c in range(NB)]
         w2_sb = [held.tile([P, C], BF16, name=f"w2_sb{c}") for c in range(NB)]
         for k in range(NB):
-            queues[k % 2].dma_start(msgs_sb[k][:], msgs[block(k), :])
-            queues[k % 2].dma_start(w_msg_sb[k][:], w_msg[block(k), :])
+            nc.sync.dma_start(msgs_sb[k][:], msgs[block(k), :])
+            nc.sync.dma_start(w_msg_sb[k][:], w_msg[block(k), :])
         for c in range(NB):
-            queues[c % 2].dma_start(ptab_sb[c][:], ptab[block(c), :])
+            nc.sync.dma_start(ptab_sb[c][:], ptab[block(c), :])
         for c in range(NB):
-            queues[c % 2].dma_start(w2_sb[c][:], w2[block(c), :])
+            nc.sync.dma_start(w2_sb[c][:], w2[block(c), :])
 
         b1_sb = held.tile([P, NB], F32, name="b1_sb")
         b2_sb = held.tile([P, NB], F32, name="b2_sb")

@@ -14,10 +14,6 @@ SILU = mybir.ActivationFunctionType.Silu
 IDENTITY = mybir.ActivationFunctionType.Identity
 
 
-def block(i):
-    return slice(i * P, (i + 1) * P)
-
-
 def tile_cartesiantransformer_kernel(tc, ptab, msgs, w_msg, b1, w2, b2, offs, out):
     nc = tc.nc
     with (
@@ -27,23 +23,24 @@ def tile_cartesiantransformer_kernel(tc, ptab, msgs, w_msg, b1, w2, b2, offs, ou
         offsets = held.tile([P, N // 16], U16, name="offsets")
         nc.sync.dma_start(offsets[:], offs)
 
-        msgs_sb = [held.tile([P, N], BF16, name=f"msgs_sb{k}") for k in range(NB)]
-        w_msg_sb = [held.tile([P, C], BF16, name=f"w_msg_sb{k}") for k in range(NB)]
-        ptab_sb = [held.tile([P, S], F32, name=f"ptab_sb{c}") for c in range(NB)]
-        w2_sb = [held.tile([P, C], BF16, name=f"w2_sb{c}") for c in range(NB)]
-        for k in range(NB):
-            nc.sync.dma_start(msgs_sb[k][:], msgs[block(k), :])
-            nc.sync.dma_start(w_msg_sb[k][:], w_msg[block(k), :])
-        for c in range(NB):
-            nc.sync.dma_start(ptab_sb[c][:], ptab[block(c), :])
-        for c in range(NB):
-            nc.sync.dma_start(w2_sb[c][:], w2[block(c), :])
-
         b1_sb = held.tile([P, NB], F32, name="b1_sb")
+        nc.sync.dma_start(b1_sb[:], b1.rearrange("(p c) o -> p (c o)", c=NB))
+        msgs_sb = held.tile([P, NB, N], BF16, name="msgs_sb")
+        nc.sync.dma_start(msgs_sb[:], msgs.rearrange("(p k) j -> p k j", k=NB))
+        w_msg_sb = held.tile([P, NB, P, NB], BF16, name="w_msg_sb")
+        nc.sync.dma_start(w_msg_sb[:], w_msg.rearrange("(p k) (q c) -> p k q c", k=NB, c=NB))
+
+        ptab_blocks = ptab.rearrange("(p c) s -> p c s", c=NB)
+        ptab_sb = [held.tile([P, S], F32, name=f"ptab_sb{c}") for c in range(NB)]
+        for c in range(NB):
+            nc.sync.dma_start(ptab_sb[c][:], ptab_blocks[:, c, :])
+
+        w2_blocks = w2.rearrange("(p c) (q m) -> p c q m", c=NB, m=NB)
+        w2_sb = [held.tile([P, P, NB], BF16, name=f"w2_sb{c}") for c in range(NB)]
+        for c in range(NB):
+            nc.sync.dma_start(w2_sb[c][:], w2_blocks[:, c, :, :])
         b2_sb = held.tile([P, NB], F32, name="b2_sb")
-        with nc.allow_non_contiguous_dma(reason="a bias of 512 values, one to a partition"):
-            nc.gpsimd.dma_start(b1_sb[:], b1.rearrange("(i p) o -> p (i o)", p=P))
-            nc.gpsimd.dma_start(b2_sb[:], b2.rearrange("(i p) o -> p (i o)", p=P))
+        nc.sync.dma_start(b2_sb[:], b2.rearrange("(p m) o -> p (m o)", m=NB))
 
         scratch = held.tile([P, 1], F32, name="scratch")
         scratch_silu = held.tile([P, 1], F32, name="scratch_silu")
@@ -51,10 +48,10 @@ def tile_cartesiantransformer_kernel(tc, ptab, msgs, w_msg, b1, w2, b2, offs, ou
         nc.scalar.activation(scratch_silu[:], scratch[:], SILU)
 
         proj = [psum.tile([P, N], F32, name=f"proj{c}") for c in range(NB)]
-        for k in range(NB):
-            for c in range(NB):
+        for c in range(NB):
+            for k in range(NB):
                 nc.tensor.matmul(
-                    proj[c][:], w_msg_sb[k][:, block(c)], msgs_sb[k][:],
+                    proj[c][:], w_msg_sb[:, k, :, c], msgs_sb[:, k, :],
                     start=(k == 0), stop=(k == NB - 1),
                 )
 
@@ -68,15 +65,16 @@ def tile_cartesiantransformer_kernel(tc, ptab, msgs, w_msg, b1, w2, b2, offs, ou
             nc.scalar.activation(hid[:], pre[:], SILU)
             for m in range(NB):
                 nc.tensor.matmul(
-                    acc[m][:], w2_sb[c][:, block(m)], hid[:],
+                    acc[m][:], w2_sb[c][:, :, m], hid[:],
                     start=(c == 0), stop=(c == NB - 1),
                 )
 
+        out_blocks = out.rearrange("(p m) j -> p m j", m=NB)
         for m in range(NB):
             out_sb = held.tile([P, N], F32, name=f"out_sb{m}")
             if m % 2 == 0:
                 nc.vector.tensor_scalar_add(out_sb[:], acc[m][:], b2_sb[:, m : m + 1])
-                nc.sync.dma_start(out[block(m), :], out_sb[:])
+                nc.sync.dma_start(out_blocks[:, m, :], out_sb[:])
             else:
                 nc.scalar.activation(out_sb[:], acc[m][:], IDENTITY, bias=b2_sb[:, m : m + 1])
-                nc.scalar.dma_start(out[block(m), :], out_sb[:])
+                nc.scalar.dma_start(out_blocks[:, m, :], out_sb[:])

@@ -5,6 +5,7 @@ C = 512
 S = 512
 N = 128
 NB = C // P
+WARM = 24
 
 FLOPS = 2 * (2 * C * C * N)
 
@@ -48,6 +49,13 @@ def tile_cartesiantransformer_kernel(tc, ptab, msgs, w_msg, b1, w2, b2, offs, ou
         nc.scalar.activation(scratch_silu[:], scratch[:], SILU)
 
         proj = [psum.tile([P, N], F32, name=f"proj{c}") for c in range(NB)]
+        acc = [psum.tile([P, N], F32, name=f"acc{m}") for m in range(NB)]
+
+        zeros = held.tile([P, N], BF16, name="zeros")
+        nc.vector.memset(zeros[:], 0.0)
+        for turn in range(WARM):
+            nc.tensor.matmul(acc[NB - 1][:], zeros[:], zeros[:], start=True, stop=True)
+
         for c in range(NB):
             for k in range(NB):
                 nc.tensor.matmul(
@@ -55,7 +63,6 @@ def tile_cartesiantransformer_kernel(tc, ptab, msgs, w_msg, b1, w2, b2, offs, ou
                     start=(k == 0), stop=(k == NB - 1),
                 )
 
-        acc = [psum.tile([P, N], F32, name=f"acc{m}") for m in range(NB)]
         for c in range(NB):
             proj_sb = held.tile([P, N], F32, name=f"proj_sb{c}")
             nc.scalar.activation(proj_sb[:], proj[c][:], IDENTITY, bias=b1_sb[:, c : c + 1])

@@ -5,7 +5,6 @@ C = 512
 S = 512
 N = 128
 NB = C // P
-WARM = 24
 
 FLOPS = 2 * (2 * C * C * N)
 
@@ -21,16 +20,17 @@ def tile_cartesiantransformer_kernel(tc, ptab, msgs, w_msg, b1, w2, b2, offs, ou
         tc.tile_pool(name="held", bufs=1) as held,
         tc.psum_pool(name="psum", bufs=1) as psum,
     ):
-        offsets = held.tile([P, N // 16], U16, name="offsets")
-        nc.sync.dma_start(offsets[:], offs)
-
         b1_sb = held.tile([P, NB], F32, name="b1_sb")
-        nc.sync.dma_start(b1_sb[:], b1.rearrange("(p c) o -> p (c o)", c=NB))
+        nc.scalar.dma_start(b1_sb[:], b1.rearrange("(p c) o -> p (c o)", c=NB))
+        b2_sb = held.tile([P, NB], F32, name="b2_sb")
+        nc.scalar.dma_start(b2_sb[:], b2.rearrange("(p m) o -> p (m o)", m=NB))
         msgs_sb = held.tile([P, NB, N], BF16, name="msgs_sb")
         nc.sync.dma_start(msgs_sb[:], msgs.rearrange("(p k) j -> p k j", k=NB))
         w_msg_sb = held.tile([P, NB, P, NB], BF16, name="w_msg_sb")
         nc.sync.dma_start(w_msg_sb[:], w_msg.rearrange("(p k) (q c) -> p k q c", k=NB, c=NB))
 
+        offsets = held.tile([P, N // 16], U16, name="offsets")
+        nc.sync.dma_start(offsets[:], offs)
         ptab_blocks = ptab.rearrange("(p c) s -> p c s", c=NB)
         ptab_sb = [held.tile([P, S], F32, name=f"ptab_sb{c}") for c in range(NB)]
         for c in range(NB):
@@ -40,8 +40,6 @@ def tile_cartesiantransformer_kernel(tc, ptab, msgs, w_msg, b1, w2, b2, offs, ou
         w2_sb = [held.tile([P, P, NB], BF16, name=f"w2_sb{c}") for c in range(NB)]
         for c in range(NB):
             nc.sync.dma_start(w2_sb[c][:], w2_blocks[:, c, :, :])
-        b2_sb = held.tile([P, NB], F32, name="b2_sb")
-        nc.sync.dma_start(b2_sb[:], b2.rearrange("(p m) o -> p (m o)", m=NB))
 
         scratch = held.tile([P, 1], F32, name="scratch")
         scratch_silu = held.tile([P, 1], F32, name="scratch_silu")
@@ -49,13 +47,6 @@ def tile_cartesiantransformer_kernel(tc, ptab, msgs, w_msg, b1, w2, b2, offs, ou
         nc.scalar.activation(scratch_silu[:], scratch[:], SILU)
 
         proj = [psum.tile([P, N], F32, name=f"proj{c}") for c in range(NB)]
-        acc = [psum.tile([P, N], F32, name=f"acc{m}") for m in range(NB)]
-
-        zeros = held.tile([P, N], BF16, name="zeros")
-        nc.vector.memset(zeros[:], 0.0)
-        for turn in range(WARM):
-            nc.tensor.matmul(acc[NB - 1][:], zeros[:], zeros[:], start=True, stop=True)
-
         for c in range(NB):
             for k in range(NB):
                 nc.tensor.matmul(
@@ -63,6 +54,7 @@ def tile_cartesiantransformer_kernel(tc, ptab, msgs, w_msg, b1, w2, b2, offs, ou
                     start=(k == 0), stop=(k == NB - 1),
                 )
 
+        acc = [psum.tile([P, N], F32, name=f"acc{m}") for m in range(NB)]
         for c in range(NB):
             proj_sb = held.tile([P, N], F32, name=f"proj_sb{c}")
             nc.scalar.activation(proj_sb[:], proj[c][:], IDENTITY, bias=b1_sb[:, c : c + 1])

@@ -22,8 +22,6 @@ def tile_cartesiantransformer_kernel(tc, ptab, msgs, w_msg, b1, w2, b2, offs, ou
     ):
         b1_sb = held.tile([P, NB], F32, name="b1_sb")
         nc.scalar.dma_start(b1_sb[:], b1.rearrange("(p c) o -> p (c o)", c=NB))
-        b2_sb = held.tile([P, NB], F32, name="b2_sb")
-        nc.scalar.dma_start(b2_sb[:], b2.rearrange("(p m) o -> p (m o)", m=NB))
         msgs_sb = held.tile([P, NB, N], BF16, name="msgs_sb")
         nc.sync.dma_start(msgs_sb[:], msgs.rearrange("(p k) j -> p k j", k=NB))
         w_msg_sb = held.tile([P, NB, P, NB], BF16, name="w_msg_sb")
@@ -40,6 +38,8 @@ def tile_cartesiantransformer_kernel(tc, ptab, msgs, w_msg, b1, w2, b2, offs, ou
         w2_sb = [held.tile([P, P, NB], BF16, name=f"w2_sb{c}") for c in range(NB)]
         for c in range(NB):
             nc.sync.dma_start(w2_sb[c][:], w2_blocks[:, c, :, :])
+        b2_sb = held.tile([P, NB], F32, name="b2_sb")
+        nc.sync.dma_start(b2_sb[:], b2.rearrange("(p m) o -> p (m o)", m=NB))
 
         scratch = held.tile([P, 1], F32, name="scratch")
         scratch_silu = held.tile([P, 1], F32, name="scratch_silu")

@@ -5,6 +5,8 @@ C = 512
 S = 512
 N = 128
 NB = C // P
+NH = 2
+NR = NB // NH
 
 FLOPS = 2 * (2 * C * C * N)
 
@@ -34,12 +36,18 @@ def tile_cartesiantransformer_kernel(tc, ptab, msgs, w_msg, b1, w2, b2, offs, ou
         for c in range(NB):
             nc.sync.dma_start(ptab_sb[c][:], ptab_blocks[:, c, :])
 
-        w2_blocks = w2.rearrange("(p c) (q m) -> p c q m", c=NB, m=NB)
-        w2_sb = [held.tile([P, P, NB], BF16, name=f"w2_sb{c}") for c in range(NB)]
-        for c in range(NB):
-            nc.sync.dma_start(w2_sb[c][:], w2_blocks[:, c, :, :])
-        b2_sb = held.tile([P, NB], F32, name="b2_sb")
-        nc.sync.dma_start(b2_sb[:], b2.rearrange("(p m) o -> p (m o)", m=NB))
+        w2_blocks = w2.rearrange("(p c) (h q r) -> p c h q r", c=NB, h=NH, r=NR)
+        w2_sb = []
+        for c in range(NB - 1):
+            w2_whole = held.tile([P, NH, P, NR], BF16, name=f"w2_whole{c}")
+            nc.sync.dma_start(w2_whole[:], w2_blocks[:, c])
+            w2_sb.append([w2_whole[:, h] for h in range(NH)])
+        w2_half = [held.tile([P, P, NR], BF16, name=f"w2_half{h}") for h in range(NH)]
+        for h in range(NH):
+            nc.sync.dma_start(w2_half[h][:], w2_blocks[:, NB - 1, h])
+        w2_sb.append([w2_half[h][:] for h in range(NH)])
+        b2_sb = held.tile([P, NH, NR], F32, name="b2_sb")
+        nc.sync.dma_start(b2_sb[:], b2.rearrange("(h q r) o -> q h (r o)", h=NH, r=NR))
 
         scratch = held.tile([P, 1], F32, name="scratch")
         scratch_silu = held.tile([P, 1], F32, name="scratch_silu")
@@ -54,7 +62,7 @@ def tile_cartesiantransformer_kernel(tc, ptab, msgs, w_msg, b1, w2, b2, offs, ou
                     start=(k == 0), stop=(k == NB - 1),
                 )
 
-        acc = [psum.tile([P, N], F32, name=f"acc{m}") for m in range(NB)]
+        acc = [[psum.tile([P, N], F32, name=f"acc{h}{r}") for r in range(NR)] for h in range(NH)]
         for c in range(NB):
             proj_sb = held.tile([P, N], F32, name=f"proj_sb{c}")
             nc.scalar.activation(proj_sb[:], proj[c][:], IDENTITY, bias=b1_sb[:, c : c + 1])
@@ -62,18 +70,16 @@ def tile_cartesiantransformer_kernel(tc, ptab, msgs, w_msg, b1, w2, b2, offs, ou
             nc.vector.tensor_tensor(pre[:], ptab_sb[c][:].indirect(offsets[:]), proj_sb[:], ADD)
             hid = held.tile([P, N], BF16, name=f"hid{c}")
             nc.scalar.activation(hid[:], pre[:], SILU)
-            for m in range(NB):
-                nc.tensor.matmul(
-                    acc[m][:], w2_sb[c][:, :, m], hid[:],
-                    start=(c == 0), stop=(c == NB - 1),
-                )
+            for h in range(NH):
+                for r in range(NR):
+                    nc.tensor.matmul(
+                        acc[h][r][:], w2_sb[c][h][:, :, r], hid[:],
+                        start=(c == 0), stop=(c == NB - 1),
+                    )
 
-        out_blocks = out.rearrange("(p m) j -> p m j", m=NB)
-        for m in range(NB):
-            out_sb = held.tile([P, N], F32, name=f"out_sb{m}")
-            if m % 2 == 0:
-                nc.vector.tensor_scalar_add(out_sb[:], acc[m][:], b2_sb[:, m : m + 1])
-                nc.sync.dma_start(out_blocks[:, m, :], out_sb[:])
-            else:
-                nc.scalar.activation(out_sb[:], acc[m][:], IDENTITY, bias=b2_sb[:, m : m + 1])
-                nc.scalar.dma_start(out_blocks[:, m, :], out_sb[:])
+        out_halves = out.rearrange("(h q r) j -> q h r j", h=NH, r=NR)
+        for h in range(NH):
+            out_sb = held.tile([P, NR, N], F32, name=f"out_sb{h}")
+            nc.vector.tensor_scalar_add(out_sb[:, 0, :], acc[h][0][:], b2_sb[:, h, 0:1])
+            nc.scalar.activation(out_sb[:, 1, :], acc[h][1][:], IDENTITY, bias=b2_sb[:, h, 1:2])
+            nc.sync.dma_start(out_halves[:, h], out_sb[:])

@@ -37,15 +37,9 @@ def tile_cartesiantransformer_kernel(tc, ptab, msgs, w_msg, b1, w2, b2, offs, ou
             nc.sync.dma_start(ptab_sb[c][:], ptab_blocks[:, c, :])
 
         w2_blocks = w2.rearrange("(p c) (h q r) -> p c h q r", c=NB, h=NH, r=NR)
-        w2_sb = []
-        for c in range(NB - 1):
-            w2_whole = held.tile([P, NH, P, NR], BF16, name=f"w2_whole{c}")
-            nc.sync.dma_start(w2_whole[:], w2_blocks[:, c])
-            w2_sb.append([w2_whole[:, h] for h in range(NH)])
-        w2_half = [held.tile([P, P, NR], BF16, name=f"w2_half{h}") for h in range(NH)]
-        for h in range(NH):
-            nc.sync.dma_start(w2_half[h][:], w2_blocks[:, NB - 1, h])
-        w2_sb.append([w2_half[h][:] for h in range(NH)])
+        w2_sb = [held.tile([P, NH, P, NR], BF16, name=f"w2_sb{c}") for c in range(NB)]
+        for c in range(NB):
+            nc.sync.dma_start(w2_sb[c][:], w2_blocks[:, c])
         b2_sb = held.tile([P, NH, NR], F32, name="b2_sb")
         nc.sync.dma_start(b2_sb[:], b2.rearrange("(h q r) o -> q h (r o)", h=NH, r=NR))
 
@@ -73,7 +67,7 @@ def tile_cartesiantransformer_kernel(tc, ptab, msgs, w_msg, b1, w2, b2, offs, ou
             for h in range(NH):
                 for r in range(NR):
                     nc.tensor.matmul(
-                        acc[h][r][:], w2_sb[c][h][:, :, r], hid[:],
+                        acc[h][r][:], w2_sb[c][:, h, :, r], hid[:],
                         start=(c == 0), stop=(c == NB - 1),
                     )
 

@@ -22,13 +22,13 @@ def tile_cartesiantransformer_kernel(tc, ptab, msgs, w_msg, b1, w2, b2, offs, ou
         tc.tile_pool(name="held", bufs=1) as held,
         tc.psum_pool(name="psum", bufs=1) as psum,
     ):
-        b1_sb = held.tile([P, NB], F32, name="b1_sb")
-        nc.scalar.dma_start(b1_sb[:], b1.rearrange("(p c) o -> p (c o)", c=NB))
         msgs_sb = held.tile([P, NB, N], BF16, name="msgs_sb")
         nc.sync.dma_start(msgs_sb[:], msgs.rearrange("(p k) j -> p k j", k=NB))
         w_msg_sb = held.tile([P, NB, P, NB], BF16, name="w_msg_sb")
         nc.sync.dma_start(w_msg_sb[:], w_msg.rearrange("(p k) (q c) -> p k q c", k=NB, c=NB))
 
+        b1_sb = held.tile([P, NB], F32, name="b1_sb")
+        nc.sync.dma_start(b1_sb[:], b1.rearrange("(p c) o -> p (c o)", c=NB))
         offsets = held.tile([P, N // 16], U16, name="offsets")
         nc.sync.dma_start(offsets[:], offs)
         ptab_blocks = ptab.rearrange("(p c) s -> p c s", c=NB)

@@ -20,6 +20,7 @@ def tile_cartesiantransformer_kernel(tc, ptab, msgs, w_msg, b1, w2, b2, offs, ou
     nc = tc.nc
     with (
         tc.tile_pool(name="held", bufs=1) as held,
+        tc.tile_pool(name="ring", bufs=3) as ring,
         tc.psum_pool(name="psum", bufs=1) as psum,
     ):
         msgs_sb = held.tile([P, NB, N], BF16, name="msgs_sb")
@@ -58,7 +59,7 @@ def tile_cartesiantransformer_kernel(tc, ptab, msgs, w_msg, b1, w2, b2, offs, ou
 
         acc = [[psum.tile([P, N], F32, name=f"acc{h}{r}") for r in range(NR)] for h in range(NH)]
         for c in range(NB):
-            proj_sb = held.tile([P, N], F32, name=f"proj_sb{c}")
+            proj_sb = ring.tile([P, N], F32, name="proj_sb")
             nc.scalar.activation(proj_sb[:], proj[c][:], IDENTITY, bias=b1_sb[:, c : c + 1])
             pre = held.tile([P, N], F32, name=f"pre{c}")
             nc.vector.tensor_tensor(pre[:], ptab_sb[c][:].indirect(offsets[:]), proj_sb[:], ADD)

import concourse.mybir as mybir

P = 128
C = 512
S = 512
N = 128
NB = C // P
NH = 2
NR = NB // NH

FLOPS = 2 * (2 * C * C * N)

BF16, F32, U16 = mybir.dt.bfloat16, mybir.dt.float32, mybir.dt.uint16
ADD = mybir.AluOpType.add
SILU = mybir.ActivationFunctionType.Silu
IDENTITY = mybir.ActivationFunctionType.Identity


def tile_cartesiantransformer_kernel(tc, ptab, msgs, w_msg, b1, w2, b2, offs, out):
    nc = tc.nc
    with (
        tc.tile_pool(name="held", bufs=1) as held,
        tc.tile_pool(name="ring", bufs=3) as ring,
        tc.psum_pool(name="psum", bufs=1) as psum,
    ):
        msgs_sb = held.tile([P, NB, N], BF16, name="msgs_sb")
        nc.sync.dma_start(msgs_sb[:], msgs.rearrange("(p k) j -> p k j", k=NB))
        w_msg_sb = held.tile([P, NB, P, NB], BF16, name="w_msg_sb")
        nc.sync.dma_start(w_msg_sb[:], w_msg.rearrange("(p k) (q c) -> p k q c", k=NB, c=NB))

        b1_sb = held.tile([P, NB], F32, name="b1_sb")
        nc.sync.dma_start(b1_sb[:], b1.rearrange("(p c) o -> p (c o)", c=NB))
        offsets = held.tile([P, N // 16], U16, name="offsets")
        nc.sync.dma_start(offsets[:], offs)
        ptab_blocks = ptab.rearrange("(p c) s -> p c s", c=NB)
        ptab_sb = [held.tile([P, S], F32, name=f"ptab_sb{c}") for c in range(NB)]
        for c in range(NB):
            nc.sync.dma_start(ptab_sb[c][:], ptab_blocks[:, c, :])

        w2_blocks = w2.rearrange("(p c) (h q r) -> p c h q r", c=NB, h=NH, r=NR)
        w2_sb = [held.tile([P, NH, P, NR], BF16, name=f"w2_sb{c}") for c in range(NB)]
        for c in range(NB):
            nc.sync.dma_start(w2_sb[c][:], w2_blocks[:, c])
        b2_sb = held.tile([P, NH, NR], F32, name="b2_sb")
        nc.sync.dma_start(b2_sb[:], b2.rearrange("(h q r) o -> q h (r o)", h=NH, r=NR))

        scratch = held.tile([P, 1], F32, name="scratch")
        scratch_silu = held.tile([P, 1], F32, name="scratch_silu")
        nc.vector.memset(scratch[:], 0.0)
        nc.scalar.activation(scratch_silu[:], scratch[:], SILU)

        proj = [psum.tile([P, N], F32, name=f"proj{c}") for c in range(NB)]
        for c in range(NB):
            for k in range(NB):
                nc.tensor.matmul(
                    proj[c][:], w_msg_sb[:, k, :, c], msgs_sb[:, k, :],
                    start=(k == 0), stop=(k == NB - 1),
                )

        acc = [[psum.tile([P, N], F32, name=f"acc{h}{r}") for r in range(NR)] for h in range(NH)]
        for c in range(NB):
            proj_sb = ring.tile([P, N], F32, name="proj_sb")
            nc.scalar.activation(proj_sb[:], proj[c][:], IDENTITY, bias=b1_sb[:, c : c + 1])
            pre = held.tile([P, N], F32, name=f"pre{c}")
            nc.vector.tensor_tensor(pre[:], ptab_sb[c][:].indirect(offsets[:]), proj_sb[:], ADD)
            hid = held.tile([P, N], BF16, name=f"hid{c}")
            nc.scalar.activation(hid[:], pre[:], SILU)
            for h in range(NH):
                for r in range(NR):
                    nc.tensor.matmul(
                        acc[h][r][:], w2_sb[c][:, h, :, r], hid[:],
                        start=(c == 0), stop=(c == NB - 1),
                    )

        out_halves = out.rearrange("(h q r) j -> q h r j", h=NH, r=NR)
        for h in range(NH):
            out_sb = held.tile([P, NR, N], F32, name=f"out_sb{h}")
            nc.vector.tensor_scalar_add(out_sb[:, 0, :], acc[h][0][:], b2_sb[:, h, 0:1])
            nc.scalar.activation(out_sb[:, 1, :], acc[h][1][:], IDENTITY, bias=b2_sb[:, h, 1:2])
            nc.sync.dma_start(out_halves[:, h], out_sb[:])
